import numpy as np
import ml_dtypes


def mxq(x, axis, fmt="e4m3"):
    dtype, down = {"e4m3": (ml_dtypes.float8_e4m3fn, 7), "e5m2": (ml_dtypes.float8_e5m2, 14)}[fmt]
    v = np.moveaxis(np.asarray(x, np.float32).astype(ml_dtypes.bfloat16).astype(np.float64), axis, -1)
    blocks = v.reshape(v.shape[:-1] + (-1, 32))
    amax = np.abs(blocks).max(-1, keepdims=True)
    byte = np.maximum(np.where(amax > 0, np.frexp(amax)[1] - 1 + 127, 0) - down, 1)
    scale = np.exp2(byte - 127.0)
    codes = (blocks / scale).astype(np.float32).astype(dtype).astype(np.float64)
    return np.moveaxis((codes * scale).reshape(v.shape), -1, axis)


WIDE = False


def mx_kscale(k):
    if not WIDE:
        return np.ones(k)
    levels = np.array([10, -10, 5, -5, 0])
    if k % 512:
        return np.exp2(np.random.permutation(np.resize(levels, k // 32))).repeat(32)
    a = np.empty((k // 512, 16))
    for p in range(k // 512):
        a[p, :8] = np.random.permutation(np.resize(levels, 8))
        for g in range(8):
            far = levels[np.abs(levels - a[p, g]) >= 10]
            a[p, g + 8] = far[np.random.randint(len(far))]
    return np.exp2(a.ravel()).repeat(32)


BF16 = ml_dtypes.bfloat16


def bf(x):
    return np.asarray(x, np.float32).astype(BF16)


def f64(x):
    return np.asarray(x).astype(np.float64)


B, N, D1, D2, F1, F2, F3, F4 = 8192, 1, 256, 256, 512, 64, 32, 16
K = D1 + D2
EPS = 1e-5
SLOPE = 0.2


def setup_inputs():
    s = mx_kscale(K)
    g = np.sqrt(EPS)
    return {"input1": bf(np.random.standard_normal((B, N, D1)) * s[:D1]),
            "input2": bf(np.random.standard_normal((B, N, D2)) * s[D1:]),
            "W1": bf(np.random.standard_normal((F1, K)) * 5.0 * g / np.sqrt(K) / s[None, :]),
            "b1": bf(np.random.standard_normal(F1) * 2.5 * g)}


def reference(input1, input2, W1, b1):
    x = np.concatenate([f64(input1), f64(input2)], axis=2)
    h = (mxq(x, 2, "e4m3") @ mxq(f64(W1), 1, "e4m3").T) + f64(b1)
    m = h.mean(axis=-1, keepdims=True)
    v = np.square(h - m).mean(axis=-1, keepdims=True)
    hn = (h - m) * (1.0 / np.sqrt(v + EPS))
    return np.where(hn >= 0, hn, SLOPE * hn)

@@ -1,0 +1,265 @@
+from contextlib import ExitStack
+
+import concourse.mybir as mybir
+from concourse.masks import make_identity
+
+FLOPS = 2 * 8192 * 512 * 512
+
+F32 = mybir.dt.float32
+BF16 = mybir.dt.bfloat16
+U32 = mybir.dt.uint32
+U8 = mybir.dt.uint8
+FP8X4 = mybir.dt.float8_e4m3fn_x4
+ALU = mybir.AluOpType
+ACT = mybir.ActivationFunctionType
+
+P = 128
+HALF = 256
+K = 2 * HALF
+F = 512
+ROW_TILES = 8192 // P
+GROUP = 4
+GROUPS = ROW_TILES // GROUP
+EPS = 1e-5
+SLOPE = 0.2
+LOAD_TILES = [4, 4, 4, 4, 8, 8, 8, 8, 8, 8]
+GPSIMD_TILES = 2
+
+
+def tile_fcd_pa_t_kernel(tc, input1, input2, W1, b1, out):
+    nc = tc.nc
+    x_views = (
+        input1.rearrange("(p t) o d -> p t (o d)", t=ROW_TILES),
+        input2.rearrange("(p t) o d -> p t (o d)", t=ROW_TILES),
+    )
+    out_view = out.rearrange("(p t) o f -> p (t o f)", t=ROW_TILES)
+    w_view = W1.rearrange("(j p) k -> p j k", p=P)
+
+    with ExitStack() as stack:
+        const = stack.enter_context(tc.tile_pool(name="const", bufs=1))
+        work = stack.enter_context(tc.tile_pool(name="work", bufs=2))
+        stats = stack.enter_context(tc.tile_pool(name="stats", bufs=8))
+        psum = stack.enter_context(tc.psum_pool(name="psum", bufs=4))
+        stack.enter_context(tc.manual_schedule())
+
+        w_words = []
+        for b in range(2):
+            w_rows = const.tile([P, 2 * K], BF16, name="w_rows%d" % b)
+            nc.sync.dma_start(
+                out=w_rows[:].rearrange("p (j k) -> p j k", j=2), in_=w_view[:, 2 * b : 2 * b + 2, :]
+            )
+            w_words.append(w_rows[:].bitcast(F32))
+        x_words = {}
+        first = 0
+        for c, n in enumerate(LOAD_TILES):
+            x_rows = const.tile([P, n * K], BF16, name="x_rows%d" % c)
+            halves = x_rows[:].rearrange("p (t s d) -> p t s d", t=n, s=2)
+            for s in range(2):
+                nc.sync.dma_start(out=halves[:, :, s, :], in_=x_views[s][:, first : first + n, :])
+            for t in range(n):
+                x_words[first + t] = (x_rows[:].bitcast(F32), t)
+            first += n
+
+        bias_row = const.tile([P, F], BF16)
+        nc.vector.memset(bias_row[:], 0.0)
+        nc.scalar.dma_start(out=bias_row[0:1, :], in_=b1.rearrange("(o f) -> o f", o=1))
+        ones = const.tile([P, P], BF16)
+        nc.vector.memset(ones[:], 1.0)
+        identity = const.tile([P, P], F32)
+        make_identity(nc, identity[:])
+        unit = const.tile([P, 1], F32)
+        nc.vector.memset(unit[:], 1.0)
+        warm = const.tile([P, 1], F32)
+        nc.scalar.activation(out=warm[:], in_=unit[:], func=ACT.Abs_reciprocal_sqrt)
+
+        def transpose_four(word_block):
+            banks = []
+            for b in range(2):
+                bank = psum.tile([P, 2, 2, P], F32, tag="words")
+                for j in range(2):
+                    for u in range(2):
+                        nc.tensor.transpose(bank[:, j, u, :], word_block(2 * b + j, u), identity[:])
+                banks.append(bank)
+            return banks
+
+        def regroup(copy, bank, grouped, b):
+            words = grouped[:].bitcast(F32).rearrange("p (j r u) -> p j r u", j=GROUP, u=2)
+            copy(out=words[:, 2 * b : 2 * b + 2, :, :], in_=bank[:].rearrange("p j u r -> p j r u"))
+
+        def w_block(j, u):
+            start = (j % 2) * HALF
+            return w_words[j // 2][:, start + u : start + HALF : 2]
+
+        w_banks = transpose_four(w_block)
+        w_grouped = const.tile([P, GROUP * K], BF16, align_bytes=64)
+        regroup(nc.vector.tensor_copy, w_banks[0], w_grouped, 0)
+        regroup(nc.vector.tensor_copy, w_banks[1], w_grouped, 1)
+        w_codes = const.tile([P, F], U32, align_bytes=64)
+        w_scales = const.tile([P, F], U8, align_bytes=64)
+        nc.vector.quantize_mx(out=w_codes[:].bitcast(FP8X4), scales=w_scales[:], in_=w_grouped[:])
+
+        banks, grouped, codes, scales, product = {}, {}, {}, {}, {}
+        hidden, row_sum, square_sum, rstd, shift, normed = {}, {}, {}, {}, {}, {}
+
+        def transpose_x(g):
+            def x_block(j, u):
+                words, t = x_words[g * GROUP + j]
+                return words[:, t * HALF + u : (t + 1) * HALF : 2]
+
+            banks[g] = transpose_four(x_block)
+
+        def regroup_x(g, b):
+            if b == 0:
+                grouped_new = work.tile([P, GROUP * K], BF16, tag="grouped", align_bytes=64)
+                grouped[g] = grouped_new
+            regroup(nc.scalar.copy, banks[g][b], grouped[g], b)
+
+        def quantise_x(g):
+            codes_new = work.tile([P, GROUP * P], U32, tag="codes", align_bytes=64)
+            scales_new = work.tile([P, GROUP * P], U8, tag="scales", align_bytes=64)
+            nc.vector.quantize_mx(
+                out=codes_new[:].bitcast(FP8X4), scales=scales_new[:], in_=grouped[g][:]
+            )
+            codes[g] = codes_new
+            scales[g] = scales_new
+
+        def multiply(g, j):
+            bank = psum.tile([P, F], F32, tag="product")
+            nc.tensor.matmul_mx(
+                out=bank[:],
+                lhsT=codes[g][:, j * P : (j + 1) * P].bitcast(FP8X4),
+                lhsT_scale=scales[g][:, j * P : (j + 1) * P],
+                rhs=w_codes[:].bitcast(FP8X4),
+                rhs_scale=w_scales[:],
+                start=True,
+                stop=True,
+            )
+            product[(g, j)] = bank
+
+        def add_bias(g, j):
+            if j == 0:
+                hidden_new = work.tile([P, GROUP, F], F32, tag="hidden", bufs=5)
+                row_sum_new = stats.tile([P, GROUP], F32, tag="row_sum")
+                hidden[g] = hidden_new
+                row_sum[g] = row_sum_new
+            nc.vector.scalar_tensor_tensor(
+                out=hidden[g][:, j, :],
+                in0=product[(g, j)][:],
+                scalar=1.0,
+                in1=bias[:],
+                op0=ALU.mult,
+                op1=ALU.add,
+                accum_out=row_sum[g][:, j : j + 1],
+            )
+
+        def sum_squares(g):
+            square_sum_new = stats.tile([P, GROUP], F32, tag="square_sum")
+            square_sum[g] = square_sum_new
+            for j in range(GROUP):
+                squares = work.tile([P, F], BF16, tag="squares")
+                nc.scalar.activation(
+                    out=squares[:],
+                    in_=hidden[g][:, j, :],
+                    func=ACT.Square,
+                    bias=row_sum[g][:, j : j + 1],
+                    scale=-1.0 * F,
+                    accum_out=square_sum[g][:, j : j + 1],
+                )
+
+        def reciprocal_std(g):
+            rstd_new = stats.tile([P, GROUP], F32, tag="rstd")
+            nc.scalar.activation(
+                out=rstd_new[:],
+                in_=square_sum[g][:],
+                func=ACT.Abs_reciprocal_sqrt,
+                bias=EPS,
+                scale=1.0 / (F * F * F),
+            )
+            rstd[g] = rstd_new
+
+        def mean_shift(g):
+            shift_new = stats.tile([P, GROUP], F32, tag="shift")
+            nc.vector.scalar_tensor_tensor(
+                out=shift_new[:],
+                in0=row_sum[g][:],
+                scalar=-1.0 / F,
+                in1=rstd[g][:],
+                op0=ALU.mult,
+                op1=ALU.mult,
+            )
+            shift[g] = shift_new
+
+        def normalise(g):
+            normed_new = work.tile([P, GROUP, F], F32, tag="normed", bufs=3)
+            normed[g] = normed_new
+            for j in range(GROUP):
+                if j < GPSIMD_TILES and g < GROUPS - 2:
+                    nc.gpsimd.tensor_scalar(
+                        out=normed[g][:, j, :],
+                        in0=hidden[g][:, j, :],
+                        scalar1=rstd[g][:, j : j + 1],
+                        scalar2=shift[g][:, j : j + 1],
+                        op0=ALU.mult,
+                        op1=ALU.add,
+                    )
+                else:
+                    nc.scalar.activation(
+                        out=normed[g][:, j, :],
+                        in_=hidden[g][:, j, :],
+                        func=ACT.Identity,
+                        bias=shift[g][:, j : j + 1],
+                        scale=rstd[g][:, j : j + 1],
+                    )
+
+        def leaky_and_store(g, pieces):
+            result = work.tile([P, GROUP * F], F32, tag="result", bufs=3)
+            width = GROUP * F // pieces
+            flat = normed[g][:].rearrange("p j f -> p (j f)")
+            for c in range(pieces):
+                cols = slice(c * width, (c + 1) * width)
+                nc.vector.scalar_tensor_tensor(
+                    out=result[:, cols],
+                    in0=flat[:, cols],
+                    scalar=SLOPE,
+                    in1=flat[:, cols],
+                    op0=ALU.mult,
+                    op1=ALU.max,
+                )
+                nc.sync.dma_start(
+                    out=out_view[:, g * GROUP * F + c * width : g * GROUP * F + (c + 1) * width],
+                    in_=result[:, cols],
+                )
+
+        transpose_x(0)
+        bias_bank = psum.tile([P, F], F32, tag="product")
+        nc.tensor.matmul(out=bias_bank[:], lhsT=ones[:], rhs=bias_row[:], start=True, stop=True)
+        bias = const.tile([P, F], F32)
+        nc.vector.tensor_copy(out=bias[:], in_=bias_bank[:])
+
+        def live(g):
+            return 0 <= g < GROUPS
+
+        for i in range(GROUPS + 6):
+            if live(i + 1):
+                transpose_x(i + 1)
+            if live(i):
+                regroup_x(i, 0)
+            if live(i - 4):
+                reciprocal_std(i - 4)
+            if live(i):
+                regroup_x(i, 1)
+            if live(i - 1):
+                quantise_x(i - 1)
+            if live(i - 5):
+                normalise(i - 5)
+            if live(i - 6):
+                leaky_and_store(i - 6, GROUP if i - 6 == GROUPS - 1 else 1)
+            if live(i - 4):
+                mean_shift(i - 4)
+            if live(i - 3):
+                sum_squares(i - 3)
+            for j in range(GROUP):
+                if live(i - 2):
+                    add_bias(i - 2, j)
+                if live(i - 1):
+                    multiply(i - 1, j)

@@ -23,7 +23,6 @@ GROUPS = ROW_TILES // GROUP
 EPS = 1e-5
 SLOPE = 0.2
 LOAD_TILES = [4, 4, 4, 4, 8, 8, 8, 8, 8, 8]
-GPSIMD_TILES = 2
 
 
 def tile_fcd_pa_t_kernel(tc, input1, input2, W1, b1, out):
@@ -99,7 +98,7 @@ def tile_fcd_pa_t_kernel(tc, input1, input2, W1, b1, out):
         nc.vector.quantize_mx(out=w_codes[:].bitcast(FP8X4), scales=w_scales[:], in_=w_grouped[:])
 
         banks, grouped, codes, scales, product = {}, {}, {}, {}, {}
-        hidden, row_sum, square_sum, rstd, shift, normed = {}, {}, {}, {}, {}, {}
+        hidden, row_sum, square_sum, rstd, shift, normed, slope = {}, {}, {}, {}, {}, {}, {}
 
         def transpose_x(g):
             def x_block(j, u):
@@ -189,11 +188,17 @@ def tile_fcd_pa_t_kernel(tc, input1, input2, W1, b1, out):
             )
             shift[g] = shift_new
 
+        def gpsimd_normalises(g, j):
+            return g < GROUPS - 2 and j < (2 if g % 2 == 0 else 1)
+
+        def gpsimd_finishes(g, j):
+            return g < GROUPS - 2 and g % 2 == 0 and j == 0
+
         def normalise(g):
             normed_new = work.tile([P, GROUP, F], F32, tag="normed", bufs=3)
             normed[g] = normed_new
             for j in range(GROUP):
-                if j < GPSIMD_TILES and g < GROUPS - 2:
+                if gpsimd_normalises(g, j):
                     nc.gpsimd.tensor_scalar(
                         out=normed[g][:, j, :],
                         in0=hidden[g][:, j, :],
@@ -202,6 +207,17 @@ def tile_fcd_pa_t_kernel(tc, input1, input2, W1, b1, out):
                         op0=ALU.mult,
                         op1=ALU.add,
                     )
+                    if gpsimd_finishes(g, j):
+                        slope_new = work.tile([P, F], F32, tag="slope")
+                        slope[g] = slope_new
+                        nc.gpsimd.tensor_scalar(
+                            out=slope[g][:],
+                            in0=normed[g][:, j, :],
+                            scalar1=0.0,
+                            scalar2=SLOPE,
+                            op0=ALU.is_ge,
+                            op1=ALU.max,
+                        )
                 else:
                     nc.scalar.activation(
                         out=normed[g][:, j, :],
@@ -211,12 +227,18 @@ def tile_fcd_pa_t_kernel(tc, input1, input2, W1, b1, out):
                         scale=rstd[g][:, j : j + 1],
                     )
 
+        def finish_tile(g):
+            finished = work.tile([P, F], F32, tag="finished")
+            nc.gpsimd.tensor_tensor(out=finished[:], in0=normed[g][:, 0, :], in1=slope[g][:], op=ALU.mult)
+            nc.sync.dma_start(out=out_view[:, g * GROUP * F : (g * GROUP + 1) * F], in_=finished[:])
+
         def leaky_and_store(g, pieces):
             result = work.tile([P, GROUP * F], F32, tag="result", bufs=3)
-            width = GROUP * F // pieces
+            start = F if gpsimd_finishes(g, 0) else 0
+            width = (GROUP * F - start) // pieces
             flat = normed[g][:].rearrange("p j f -> p (j f)")
             for c in range(pieces):
-                cols = slice(c * width, (c + 1) * width)
+                cols = slice(start + c * width, start + (c + 1) * width)
                 nc.vector.scalar_tensor_tensor(
                     out=result[:, cols],
                     in0=flat[:, cols],
@@ -226,7 +248,7 @@ def tile_fcd_pa_t_kernel(tc, input1, input2, W1, b1, out):
                     op1=ALU.max,
                 )
                 nc.sync.dma_start(
-                    out=out_view[:, g * GROUP * F + c * width : g * GROUP * F + (c + 1) * width],
+                    out=out_view[:, g * GROUP * F + cols.start : g * GROUP * F + cols.stop],
                     in_=result[:, cols],
                 )
 
@@ -254,6 +276,8 @@ def tile_fcd_pa_t_kernel(tc, input1, input2, W1, b1, out):
                 normalise(i - 5)
             if live(i - 6):
                 leaky_and_store(i - 6, GROUP if i - 6 == GROUPS - 1 else 1)
+                if gpsimd_finishes(i - 6, 0):
+                    finish_tile(i - 6)
             if live(i - 4):
                 mean_shift(i - 4)
             if live(i - 3):

@@ -98,7 +98,7 @@ def tile_fcd_pa_t_kernel(tc, input1, input2, W1, b1, out):
         nc.vector.quantize_mx(out=w_codes[:].bitcast(FP8X4), scales=w_scales[:], in_=w_grouped[:])
 
         banks, grouped, codes, scales, product = {}, {}, {}, {}, {}
-        hidden, row_sum, square_sum, rstd, shift, normed, slope = {}, {}, {}, {}, {}, {}, {}
+        hidden, row_sum, square_sum, rstd, shift, normed, lift = {}, {}, {}, {}, {}, {}, {}
 
         def transpose_x(g):
             def x_block(j, u):
@@ -189,7 +189,7 @@ def tile_fcd_pa_t_kernel(tc, input1, input2, W1, b1, out):
             shift[g] = shift_new
 
         def gpsimd_normalises(g, j):
-            return g < GROUPS - 2 and j < (2 if g % 2 == 0 else 1)
+            return g < GROUPS - 2 and j < (3 if g % 2 == 0 else 1)
 
         def gpsimd_finishes(g, j):
             return g < GROUPS - 2 and g % 2 == 0 and j == 0
@@ -207,17 +207,6 @@ def tile_fcd_pa_t_kernel(tc, input1, input2, W1, b1, out):
                         op0=ALU.mult,
                         op1=ALU.add,
                     )
-                    if gpsimd_finishes(g, j):
-                        slope_new = work.tile([P, F], F32, tag="slope")
-                        slope[g] = slope_new
-                        nc.gpsimd.tensor_scalar(
-                            out=slope[g][:],
-                            in0=normed[g][:, j, :],
-                            scalar1=0.0,
-                            scalar2=SLOPE,
-                            op0=ALU.is_ge,
-                            op1=ALU.max,
-                        )
                 else:
                     nc.scalar.activation(
                         out=normed[g][:, j, :],
@@ -226,10 +215,16 @@ def tile_fcd_pa_t_kernel(tc, input1, input2, W1, b1, out):
                         bias=shift[g][:, j : j + 1],
                         scale=rstd[g][:, j : j + 1],
                     )
+            if gpsimd_finishes(g, 0):
+                lift_new = work.tile([P, F], F32, tag="lift")
+                lift[g] = lift_new
+                nc.scalar.activation(
+                    out=lift[g][:], in_=normed[g][:, 0, :], func=ACT.Relu, scale=-(1.0 - SLOPE)
+                )
 
         def finish_tile(g):
             finished = work.tile([P, F], F32, tag="finished")
-            nc.gpsimd.tensor_tensor(out=finished[:], in0=normed[g][:, 0, :], in1=slope[g][:], op=ALU.mult)
+            nc.gpsimd.tensor_tensor(out=finished[:], in0=normed[g][:, 0, :], in1=lift[g][:], op=ALU.add)
             nc.sync.dma_start(out=out_view[:, g * GROUP * F : (g * GROUP + 1) * F], in_=finished[:])
 
         def leaky_and_store(g, pieces):

@@ -17,12 +17,15 @@ P = 128
 HALF = 256
 K = 2 * HALF
 F = 512
+F_TILES = F // P
 ROW_TILES = 8192 // P
-GROUP = 4
-GROUPS = ROW_TILES // GROUP
 EPS = 1e-5
 SLOPE = 0.2
-LOAD_TILES = [4, 4, 4, 4, 8, 8, 8, 8, 8, 8]
+SIZES = [2, 2] + [4] * 14 + [2, 2]
+GROUPS = len(SIZES)
+FIRST = [sum(SIZES[:g]) for g in range(GROUPS)]
+LOAD_TILES = SIZES[:9] + [8] * 4
+LAST_GROUPS = 4
 
 
 def tile_fcd_pa_t_kernel(tc, input1, input2, W1, b1, out):
@@ -41,81 +44,67 @@ def tile_fcd_pa_t_kernel(tc, input1, input2, W1, b1, out):
         psum = stack.enter_context(tc.psum_pool(name="psum", bufs=4))
         stack.enter_context(tc.manual_schedule())
 
-        w_words = []
-        for b in range(2):
-            w_rows = const.tile([P, 2 * K], BF16, name="w_rows%d" % b)
-            nc.sync.dma_start(
-                out=w_rows[:].rearrange("p (j k) -> p j k", j=2), in_=w_view[:, 2 * b : 2 * b + 2, :]
-            )
-            w_words.append(w_rows[:].bitcast(F32))
         x_words = {}
-        first = 0
-        for c, n in enumerate(LOAD_TILES):
+
+        def load_x(c):
+            n = LOAD_TILES[c]
+            first = sum(LOAD_TILES[:c])
             x_rows = const.tile([P, n * K], BF16, name="x_rows%d" % c)
             halves = x_rows[:].rearrange("p (t s d) -> p t s d", t=n, s=2)
             for s in range(2):
                 nc.sync.dma_start(out=halves[:, :, s, :], in_=x_views[s][:, first : first + n, :])
             for t in range(n):
                 x_words[first + t] = (x_rows[:].bitcast(F32), t)
-            first += n
+
+        load_x(0)
+        w_words = []
+        for j in range(F_TILES):
+            w_rows = const.tile([P, K], BF16, name="w_rows%d" % j)
+            nc.sync.dma_start(out=w_rows[:], in_=w_view[:, j, :])
+            w_words.append(w_rows[:].bitcast(F32))
+        for c in range(1, len(LOAD_TILES)):
+            load_x(c)
 
         bias_row = const.tile([P, F], BF16)
         nc.vector.memset(bias_row[:], 0.0)
         nc.scalar.dma_start(out=bias_row[0:1, :], in_=b1.rearrange("(o f) -> o f", o=1))
+        unit = const.tile([P, 1], F32)
+        nc.vector.memset(unit[:], 1.0)
         ones = const.tile([P, P], BF16)
         nc.vector.memset(ones[:], 1.0)
         identity = const.tile([P, P], F32)
         make_identity(nc, identity[:])
-        unit = const.tile([P, 1], F32)
-        nc.vector.memset(unit[:], 1.0)
         warm = const.tile([P, 1], F32)
         nc.scalar.activation(out=warm[:], in_=unit[:], func=ACT.Abs_reciprocal_sqrt)
 
-        def transpose_four(word_block):
-            banks = []
-            for b in range(2):
+        banks, grouped, codes, scales, product = {}, {}, {}, {}, {}
+        hidden, row_sum, square_sum, rstd, shift, normed = {}, {}, {}, {}, {}, {}
+        lift, finished = {}, {}
+
+        def transpose(g):
+            for b in range(SIZES[g] // 2):
                 bank = psum.tile([P, 2, 2, P], F32, tag="words")
                 for j in range(2):
+                    words, t = x_words[FIRST[g] + 2 * b + j]
                     for u in range(2):
-                        nc.tensor.transpose(bank[:, j, u, :], word_block(2 * b + j, u), identity[:])
-                banks.append(bank)
-            return banks
+                        nc.tensor.transpose(
+                            bank[:, j, u, :], words[:, t * HALF + u : (t + 1) * HALF : 2], identity[:]
+                        )
+                banks[(g, b)] = bank
 
-        def regroup(copy, bank, grouped, b):
-            words = grouped[:].bitcast(F32).rearrange("p (j r u) -> p j r u", j=GROUP, u=2)
-            copy(out=words[:, 2 * b : 2 * b + 2, :, :], in_=bank[:].rearrange("p j u r -> p j r u"))
-
-        def w_block(j, u):
-            start = (j % 2) * HALF
-            return w_words[j // 2][:, start + u : start + HALF : 2]
-
-        w_banks = transpose_four(w_block)
-        w_grouped = const.tile([P, GROUP * K], BF16, align_bytes=64)
-        regroup(nc.vector.tensor_copy, w_banks[0], w_grouped, 0)
-        regroup(nc.vector.tensor_copy, w_banks[1], w_grouped, 1)
-        w_codes = const.tile([P, F], U32, align_bytes=64)
-        w_scales = const.tile([P, F], U8, align_bytes=64)
-        nc.vector.quantize_mx(out=w_codes[:].bitcast(FP8X4), scales=w_scales[:], in_=w_grouped[:])
-
-        banks, grouped, codes, scales, product = {}, {}, {}, {}, {}
-        hidden, row_sum, square_sum, rstd, shift, normed, lift = {}, {}, {}, {}, {}, {}, {}
-
-        def transpose_x(g):
-            def x_block(j, u):
-                words, t = x_words[g * GROUP + j]
-                return words[:, t * HALF + u : (t + 1) * HALF : 2]
-
-            banks[g] = transpose_four(x_block)
-
-        def regroup_x(g, b):
+        def regroup(g, b):
             if b == 0:
-                grouped_new = work.tile([P, GROUP * K], BF16, tag="grouped", align_bytes=64)
+                grouped_new = work.tile([P, SIZES[g] * K], BF16, tag="grouped", align_bytes=64)
                 grouped[g] = grouped_new
-            regroup(nc.scalar.copy, banks[g][b], grouped[g], b)
+            words = grouped[g][:].bitcast(F32).rearrange("p (j r u) -> p j r u", j=SIZES[g], u=2)
+            nc.scalar.copy(
+                out=words[:, 2 * b : 2 * b + 2, :, :],
+                in_=banks[(g, b)][:].rearrange("p j u r -> p j r u"),
+            )
 
-        def quantise_x(g):
-            codes_new = work.tile([P, GROUP * P], U32, tag="codes", align_bytes=64)
-            scales_new = work.tile([P, GROUP * P], U8, tag="scales", align_bytes=64)
+        def quantise(g):
+            codes_new = work.tile([P, SIZES[g] * P], U32, tag="codes", align_bytes=64)
+            scales_new = work.tile([P, SIZES[g] * P], U8, tag="scales", align_bytes=64)
             nc.vector.quantize_mx(
                 out=codes_new[:].bitcast(FP8X4), scales=scales_new[:], in_=grouped[g][:]
             )
@@ -137,8 +126,8 @@ def tile_fcd_pa_t_kernel(tc, input1, input2, W1, b1, out):
 
         def add_bias(g, j):
             if j == 0:
-                hidden_new = work.tile([P, GROUP, F], F32, tag="hidden", bufs=5)
-                row_sum_new = stats.tile([P, GROUP], F32, tag="row_sum")
+                hidden_new = work.tile([P, SIZES[g], F], F32, tag="hidden", bufs=5)
+                row_sum_new = stats.tile([P, SIZES[g]], F32, tag="row_sum")
                 hidden[g] = hidden_new
                 row_sum[g] = row_sum_new
             nc.vector.scalar_tensor_tensor(
@@ -152,9 +141,9 @@ def tile_fcd_pa_t_kernel(tc, input1, input2, W1, b1, out):
             )
 
         def sum_squares(g):
-            square_sum_new = stats.tile([P, GROUP], F32, tag="square_sum")
+            square_sum_new = stats.tile([P, SIZES[g]], F32, tag="square_sum")
             square_sum[g] = square_sum_new
-            for j in range(GROUP):
+            for j in range(SIZES[g]):
                 squares = work.tile([P, F], BF16, tag="squares")
                 nc.scalar.activation(
                     out=squares[:],
@@ -166,7 +155,7 @@ def tile_fcd_pa_t_kernel(tc, input1, input2, W1, b1, out):
                 )
 
         def reciprocal_std(g):
-            rstd_new = stats.tile([P, GROUP], F32, tag="rstd")
+            rstd_new = stats.tile([P, SIZES[g]], F32, tag="rstd")
             nc.scalar.activation(
                 out=rstd_new[:],
                 in_=square_sum[g][:],
@@ -177,7 +166,7 @@ def tile_fcd_pa_t_kernel(tc, input1, input2, W1, b1, out):
             rstd[g] = rstd_new
 
         def mean_shift(g):
-            shift_new = stats.tile([P, GROUP], F32, tag="shift")
+            shift_new = stats.tile([P, SIZES[g]], F32, tag="shift")
             nc.vector.scalar_tensor_tensor(
                 out=shift_new[:],
                 in0=row_sum[g][:],
@@ -188,52 +177,61 @@ def tile_fcd_pa_t_kernel(tc, input1, input2, W1, b1, out):
             )
             shift[g] = shift_new
 
-        def gpsimd_normalises(g, j):
-            return g < GROUPS - 2 and j < (3 if g % 2 == 0 else 1)
+        def gpsimd_tiles(g):
+            if SIZES[g] < 4 or g >= GROUPS - LAST_GROUPS:
+                return 0
+            return 3 if g % 2 == 0 else 1
 
-        def gpsimd_finishes(g, j):
-            return g < GROUPS - 2 and g % 2 == 0 and j == 0
+        def gpsimd_finishes(g):
+            return gpsimd_tiles(g) == 3
 
-        def normalise(g):
-            normed_new = work.tile([P, GROUP, F], F32, tag="normed", bufs=3)
+        def normalise_gpsimd(g):
+            normed_new = work.tile([P, SIZES[g], F], F32, tag="normed", bufs=4)
             normed[g] = normed_new
-            for j in range(GROUP):
-                if gpsimd_normalises(g, j):
-                    nc.gpsimd.tensor_scalar(
-                        out=normed[g][:, j, :],
-                        in0=hidden[g][:, j, :],
-                        scalar1=rstd[g][:, j : j + 1],
-                        scalar2=shift[g][:, j : j + 1],
-                        op0=ALU.mult,
-                        op1=ALU.add,
-                    )
-                else:
-                    nc.scalar.activation(
-                        out=normed[g][:, j, :],
-                        in_=hidden[g][:, j, :],
-                        func=ACT.Identity,
-                        bias=shift[g][:, j : j + 1],
-                        scale=rstd[g][:, j : j + 1],
-                    )
-            if gpsimd_finishes(g, 0):
-                lift_new = work.tile([P, F], F32, tag="lift")
-                lift[g] = lift_new
-                nc.scalar.activation(
-                    out=lift[g][:], in_=normed[g][:, 0, :], func=ACT.Relu, scale=-(1.0 - SLOPE)
+            for j in range(gpsimd_tiles(g)):
+                nc.gpsimd.tensor_scalar(
+                    out=normed[g][:, j, :],
+                    in0=hidden[g][:, j, :],
+                    scalar1=rstd[g][:, j : j + 1],
+                    scalar2=shift[g][:, j : j + 1],
+                    op0=ALU.mult,
+                    op1=ALU.add,
                 )
 
-        def finish_tile(g):
-            finished = work.tile([P, F], F32, tag="finished")
-            nc.gpsimd.tensor_tensor(out=finished[:], in0=normed[g][:, 0, :], in1=lift[g][:], op=ALU.add)
-            nc.sync.dma_start(out=out_view[:, g * GROUP * F : (g * GROUP + 1) * F], in_=finished[:])
+        def normalise_scalar(g):
+            for j in range(gpsimd_tiles(g), SIZES[g]):
+                nc.scalar.activation(
+                    out=normed[g][:, j, :],
+                    in_=hidden[g][:, j, :],
+                    func=ACT.Identity,
+                    bias=shift[g][:, j : j + 1],
+                    scale=rstd[g][:, j : j + 1],
+                )
 
-        def leaky_and_store(g, pieces):
-            result = work.tile([P, GROUP * F], F32, tag="result", bufs=3)
-            start = F if gpsimd_finishes(g, 0) else 0
-            width = (GROUP * F - start) // pieces
+        def lift_negatives(g):
+            lift_new = work.tile([P, F], F32, tag="lift")
+            lift[g] = lift_new
+            nc.scalar.activation(
+                out=lift[g][:], in_=normed[g][:, 0, :], func=ACT.Relu, scale=-(1.0 - SLOPE)
+            )
+
+        def finish_tile(g):
+            finished_new = work.tile([P, F], F32, tag="finished")
+            finished[g] = finished_new
+            nc.gpsimd.tensor_tensor(
+                out=finished[g][:], in0=normed[g][:, 0, :], in1=lift[g][:], op=ALU.add
+            )
+
+        def store(source, first, n):
+            nc.sync.dma_start(out=out_view[:, first * F : (first + n) * F], in_=source)
+
+        def leaky_and_store(g):
+            result = work.tile([P, SIZES[g] * F], F32, tag="result", bufs=4)
             flat = normed[g][:].rearrange("p j f -> p (j f)")
-            for c in range(pieces):
-                cols = slice(start + c * width, start + (c + 1) * width)
+            start = 1 if gpsimd_finishes(g) else 0
+            step = 1 if g >= GROUPS - LAST_GROUPS else SIZES[g] - start
+            for j in range(start, SIZES[g], step):
+                cols = slice(j * F, (j + step) * F)
                 nc.vector.scalar_tensor_tensor(
                     out=result[:, cols],
                     in0=flat[:, cols],
@@ -242,43 +240,67 @@ def tile_fcd_pa_t_kernel(tc, input1, input2, W1, b1, out):
                     op0=ALU.mult,
                     op1=ALU.max,
                 )
-                nc.sync.dma_start(
-                    out=out_view[:, g * GROUP * F + cols.start : g * GROUP * F + cols.stop],
-                    in_=result[:, cols],
-                )
+                store(result[:, cols], FIRST[g] + j, step)
 
-        transpose_x(0)
+        transpose(0)
         bias_bank = psum.tile([P, F], F32, tag="product")
         nc.tensor.matmul(out=bias_bank[:], lhsT=ones[:], rhs=bias_row[:], start=True, stop=True)
         bias = const.tile([P, F], F32)
         nc.vector.tensor_copy(out=bias[:], in_=bias_bank[:])
+        regroup(0, 0)
+        quantise(0)
+        w_codes = const.tile([P, F], U32, align_bytes=64)
+        w_scales = const.tile([P, F], U8, align_bytes=64)
+        for j in range(F_TILES):
+            w_bank = psum.tile([P, 2, P], F32, tag="words")
+            for u in range(2):
+                nc.tensor.transpose(w_bank[:, u, :], w_words[j][:, u::2], identity[:])
+            w_grouped = work.tile([P, K], BF16, tag="w_grouped", align_bytes=64)
+            nc.scalar.copy(
+                out=w_grouped[:].bitcast(F32).rearrange("p (r u) -> p r u", u=2),
+                in_=w_bank[:].rearrange("p u r -> p r u"),
+            )
+            cols = slice(j * P, (j + 1) * P)
+            nc.vector.quantize_mx(
+                out=w_codes[:, cols].bitcast(FP8X4), scales=w_scales[:, cols], in_=w_grouped[:]
+            )
+        transpose(1)
 
         def live(g):
             return 0 <= g < GROUPS
 
-        for i in range(GROUPS + 6):
-            if live(i + 1):
-                transpose_x(i + 1)
-            if live(i):
-                regroup_x(i, 0)
+        transposed = 2
+        for i in range(GROUPS + 8):
+            if live(i) and i > 0:
+                regroup(i, 0)
             if live(i - 4):
                 reciprocal_std(i - 4)
-            if live(i):
-                regroup_x(i, 1)
-            if live(i - 1):
-                quantise_x(i - 1)
             if live(i - 5):
-                normalise(i - 5)
+                normalise_gpsimd(i - 5)
+                if gpsimd_finishes(i - 5):
+                    lift_negatives(i - 5)
+            if live(i) and SIZES[i] > 2:
+                regroup(i, 1)
+            if live(i - 1) and i > 1:
+                quantise(i - 1)
+            if live(i - 5):
+                normalise_scalar(i - 5)
             if live(i - 6):
-                leaky_and_store(i - 6, GROUP if i - 6 == GROUPS - 1 else 1)
-                if gpsimd_finishes(i - 6, 0):
+                leaky_and_store(i - 6)
+                if gpsimd_finishes(i - 6):
                     finish_tile(i - 6)
+            if live(i - 7) and gpsimd_finishes(i - 7):
+                store(finished[i - 7][:], FIRST[i - 7], 1)
             if live(i - 4):
                 mean_shift(i - 4)
             if live(i - 3):
                 sum_squares(i - 3)
-            for j in range(GROUP):
-                if live(i - 2):
+            for j in range(4):
+                if live(i - 2) and j < SIZES[i - 2]:
                     add_bias(i - 2, j)
-                if live(i - 1):
+                if live(i - 1) and j < SIZES[i - 1]:
                     multiply(i - 1, j)
+            if i >= 1:
+                while transposed < min(i + 3, GROUPS):
+                    transpose(transposed)
+                    transposed += 1

@@ -125,7 +125,7 @@ def tile_fcd_pa_t_kernel(tc, input1, input2, W1, b1, out):
             product[(g, j)] = bank
 
         def add_bias(g, j):
-            if j == 0:
+            if g not in hidden:
                 hidden_new = work.tile([P, SIZES[g], F], F32, tag="hidden", bufs=5)
                 row_sum_new = stats.tile([P, SIZES[g]], F32, tag="row_sum")
                 hidden[g] = hidden_new
@@ -143,7 +143,7 @@ def tile_fcd_pa_t_kernel(tc, input1, input2, W1, b1, out):
         def sum_squares(g):
             square_sum_new = stats.tile([P, SIZES[g]], F32, tag="square_sum")
             square_sum[g] = square_sum_new
-            for j in range(SIZES[g]):
+            for j in [SIZES[g] - 2, SIZES[g] - 1] + list(range(SIZES[g] - 2)):
                 squares = work.tile([P, F], BF16, tag="squares")
                 nc.scalar.activation(
                     out=squares[:],
@@ -281,8 +281,6 @@ def tile_fcd_pa_t_kernel(tc, input1, input2, W1, b1, out):
                     lift_negatives(i - 5)
             if live(i) and SIZES[i] > 2:
                 regroup(i, 1)
-            if live(i - 1) and i > 1:
-                quantise(i - 1)
             if live(i - 5):
                 normalise_scalar(i - 5)
             if live(i - 6):
@@ -291,12 +289,16 @@ def tile_fcd_pa_t_kernel(tc, input1, input2, W1, b1, out):
                     finish_tile(i - 6)
             if live(i - 7) and gpsimd_finishes(i - 7):
                 store(finished[i - 7][:], FIRST[i - 7], 1)
+            if live(i - 1) and i > 1:
+                quantise(i - 1)
             if live(i - 4):
                 mean_shift(i - 4)
             if live(i - 3):
                 sum_squares(i - 3)
+            if live(i - 2):
+                add_bias(i - 2, SIZES[i - 2] - 1)
             for j in range(4):
-                if live(i - 2) and j < SIZES[i - 2]:
+                if live(i - 2) and j < SIZES[i - 2] - 1:
                     add_bias(i - 2, j)
                 if live(i - 1) and j < SIZES[i - 1]:
                     multiply(i - 1, j)

@@ -25,7 +25,9 @@ SIZES = [2, 2] + [4] * 14 + [2, 2]
 GROUPS = len(SIZES)
 FIRST = [sum(SIZES[:g]) for g in range(GROUPS)]
 LOAD_TILES = SIZES[:9] + [8] * 4
-LAST_GROUPS = 4
+LAST_GROUPS = 5
+FILLING = 3
+WARM_UPS = 5
 
 
 def tile_fcd_pa_t_kernel(tc, input1, input2, W1, b1, out):
@@ -65,13 +67,13 @@ def tile_fcd_pa_t_kernel(tc, input1, input2, W1, b1, out):
         for c in range(1, len(LOAD_TILES)):
             load_x(c)
 
+        ones = const.tile([P, F], BF16)
+        nc.vector.memset(ones[:], 1.0)
         bias_row = const.tile([P, F], BF16)
         nc.vector.memset(bias_row[:], 0.0)
         nc.scalar.dma_start(out=bias_row[0:1, :], in_=b1.rearrange("(o f) -> o f", o=1))
         unit = const.tile([P, 1], F32)
         nc.vector.memset(unit[:], 1.0)
-        ones = const.tile([P, P], BF16)
-        nc.vector.memset(ones[:], 1.0)
         identity = const.tile([P, P], F32)
         make_identity(nc, identity[:])
         warm = const.tile([P, 1], F32)
@@ -124,6 +126,10 @@ def tile_fcd_pa_t_kernel(tc, input1, input2, W1, b1, out):
             )
             product[(g, j)] = bank
 
+        def bias_add_order(g):
+            tiles = list(range(SIZES[g]))
+            return tiles if g < FILLING else tiles[-1:] + tiles[:-1]
+
         def add_bias(g, j):
             if g not in hidden:
                 hidden_new = work.tile([P, SIZES[g], F], F32, tag="hidden", bufs=5)
@@ -143,7 +149,8 @@ def tile_fcd_pa_t_kernel(tc, input1, input2, W1, b1, out):
         def sum_squares(g):
             square_sum_new = stats.tile([P, SIZES[g]], F32, tag="square_sum")
             square_sum[g] = square_sum_new
-            for j in [SIZES[g] - 2, SIZES[g] - 1] + list(range(SIZES[g] - 2)):
+            order = bias_add_order(g)
+            for j in order[-1:] + order[:-1]:
                 squares = work.tile([P, F], BF16, tag="squares")
                 nc.scalar.activation(
                     out=squares[:],
@@ -178,7 +185,7 @@ def tile_fcd_pa_t_kernel(tc, input1, input2, W1, b1, out):
             shift[g] = shift_new
 
         def gpsimd_tiles(g):
-            if SIZES[g] < 4 or g >= GROUPS - LAST_GROUPS:
+            if SIZES[g] < 4 or g >= GROUPS - 4:
                 return 0
             return 3 if g % 2 == 0 else 1
 
@@ -242,9 +249,13 @@ def tile_fcd_pa_t_kernel(tc, input1, input2, W1, b1, out):
                 )
                 store(result[:, cols], FIRST[g] + j, step)
 
-        transpose(0)
         bias_bank = psum.tile([P, F], F32, tag="product")
-        nc.tensor.matmul(out=bias_bank[:], lhsT=ones[:], rhs=bias_row[:], start=True, stop=True)
+        for n in range(WARM_UPS):
+            nc.tensor.matmul(out=bias_bank[:], lhsT=ones[:, 0:P], rhs=ones[:], start=True, stop=True)
+        transpose(0)
+        nc.tensor.matmul(
+            out=bias_bank[:], lhsT=ones[:, 0:P], rhs=bias_row[:], start=True, stop=True
+        )
         bias = const.tile([P, F], F32)
         nc.vector.tensor_copy(out=bias[:], in_=bias_bank[:])
         regroup(0, 0)
@@ -289,16 +300,17 @@ def tile_fcd_pa_t_kernel(tc, input1, input2, W1, b1, out):
                     finish_tile(i - 6)
             if live(i - 7) and gpsimd_finishes(i - 7):
                 store(finished[i - 7][:], FIRST[i - 7], 1)
-            if live(i - 1) and i > 1:
-                quantise(i - 1)
             if live(i - 4):
                 mean_shift(i - 4)
+            if live(i - 1) and i > 1:
+                quantise(i - 1)
             if live(i - 3):
                 sum_squares(i - 3)
-            if live(i - 2):
-                add_bias(i - 2, SIZES[i - 2] - 1)
+            order = bias_add_order(i - 2) if live(i - 2) else []
+            if order and order[0] != 0:
+                add_bias(i - 2, order[0])
             for j in range(4):
-                if live(i - 2) and j < SIZES[i - 2] - 1:
+                if j in order and (j != order[0] or j == 0):
                     add_bias(i - 2, j)
                 if live(i - 1) and j < SIZES[i - 1]:
                     multiply(i - 1, j)

@@ -27,7 +27,7 @@ FIRST = [sum(SIZES[:g]) for g in range(GROUPS)]
 LOAD_TILES = SIZES[:9] + [8] * 4
 LAST_GROUPS = 5
 FILLING = 3
-WARM_UPS = 5
+WARM_UPS = 3
 
 
 def tile_fcd_pa_t_kernel(tc, input1, input2, W1, b1, out):
@@ -229,16 +229,20 @@ def tile_fcd_pa_t_kernel(tc, input1, input2, W1, b1, out):
                 out=finished[g][:], in0=normed[g][:, 0, :], in1=lift[g][:], op=ALU.add
             )
 
-        def store(source, first, n):
-            nc.sync.dma_start(out=out_view[:, first * F : (first + n) * F], in_=source)
+        def store(source, g, start, stop):
+            nc.sync.dma_start(out=out_view[:, FIRST[g] * F + start : FIRST[g] * F + stop], in_=source)
 
         def leaky_and_store(g):
             result = work.tile([P, SIZES[g] * F], F32, tag="result", bufs=4)
             flat = normed[g][:].rearrange("p j f -> p (j f)")
-            start = 1 if gpsimd_finishes(g) else 0
-            step = 1 if g >= GROUPS - LAST_GROUPS else SIZES[g] - start
-            for j in range(start, SIZES[g], step):
-                cols = slice(j * F, (j + step) * F)
+            start = F if gpsimd_finishes(g) else 0
+            width = SIZES[g] * F - start
+            if g >= GROUPS - LAST_GROUPS:
+                width = F
+            if g == GROUPS - 1:
+                width = F // 2
+            for c in range(start, SIZES[g] * F, width):
+                cols = slice(c, c + width)
                 nc.vector.scalar_tensor_tensor(
                     out=result[:, cols],
                     in0=flat[:, cols],
@@ -247,17 +251,12 @@ def tile_fcd_pa_t_kernel(tc, input1, input2, W1, b1, out):
                     op0=ALU.mult,
                     op1=ALU.max,
                 )
-                store(result[:, cols], FIRST[g] + j, step)
+                store(result[:, cols], g, c, c + width)
 
         bias_bank = psum.tile([P, F], F32, tag="product")
         for n in range(WARM_UPS):
             nc.tensor.matmul(out=bias_bank[:], lhsT=ones[:, 0:P], rhs=ones[:], start=True, stop=True)
         transpose(0)
-        nc.tensor.matmul(
-            out=bias_bank[:], lhsT=ones[:, 0:P], rhs=bias_row[:], start=True, stop=True
-        )
-        bias = const.tile([P, F], F32)
-        nc.vector.tensor_copy(out=bias[:], in_=bias_bank[:])
         regroup(0, 0)
         quantise(0)
         w_codes = const.tile([P, F], U32, align_bytes=64)
@@ -275,12 +274,18 @@ def tile_fcd_pa_t_kernel(tc, input1, input2, W1, b1, out):
             nc.vector.quantize_mx(
                 out=w_codes[:, cols].bitcast(FP8X4), scales=w_scales[:, cols], in_=w_grouped[:]
             )
+        nc.tensor.matmul(
+            out=bias_bank[:], lhsT=ones[:, 0:P], rhs=bias_row[:], start=True, stop=True
+        )
+        bias = const.tile([P, F], F32)
+        nc.vector.tensor_copy(out=bias[:], in_=bias_bank[:])
         transpose(1)
+        transpose(2)
 
         def live(g):
             return 0 <= g < GROUPS
 
-        transposed = 2
+        transposed = 3
         for i in range(GROUPS + 8):
             if live(i) and i > 0:
                 regroup(i, 0)
@@ -299,7 +304,7 @@ def tile_fcd_pa_t_kernel(tc, input1, input2, W1, b1, out):
                 if gpsimd_finishes(i - 6):
                     finish_tile(i - 6)
             if live(i - 7) and gpsimd_finishes(i - 7):
-                store(finished[i - 7][:], FIRST[i - 7], 1)
+                store(finished[i - 7][:], i - 7, 0, F)
             if live(i - 4):
                 mean_shift(i - 4)
             if live(i - 1) and i > 1:

from contextlib import ExitStack

import concourse.mybir as mybir
from concourse.masks import make_identity

FLOPS = 2 * 8192 * 512 * 512

F32 = mybir.dt.float32
BF16 = mybir.dt.bfloat16
U32 = mybir.dt.uint32
U8 = mybir.dt.uint8
FP8X4 = mybir.dt.float8_e4m3fn_x4
ALU = mybir.AluOpType
ACT = mybir.ActivationFunctionType

P = 128
HALF = 256
K = 2 * HALF
F = 512
F_TILES = F // P
ROW_TILES = 8192 // P
EPS = 1e-5
SLOPE = 0.2
SIZES = [2, 2] + [4] * 14 + [2, 2]
GROUPS = len(SIZES)
FIRST = [sum(SIZES[:g]) for g in range(GROUPS)]
LOAD_TILES = SIZES[:9] + [8] * 4
LAST_GROUPS = 5
FILLING = 3
WARM_UPS = 3


def tile_fcd_pa_t_kernel(tc, input1, input2, W1, b1, out):
    nc = tc.nc
    x_views = (
        input1.rearrange("(p t) o d -> p t (o d)", t=ROW_TILES),
        input2.rearrange("(p t) o d -> p t (o d)", t=ROW_TILES),
    )
    out_view = out.rearrange("(p t) o f -> p (t o f)", t=ROW_TILES)
    w_view = W1.rearrange("(j p) k -> p j k", p=P)

    with ExitStack() as stack:
        const = stack.enter_context(tc.tile_pool(name="const", bufs=1))
        work = stack.enter_context(tc.tile_pool(name="work", bufs=2))
        stats = stack.enter_context(tc.tile_pool(name="stats", bufs=8))
        psum = stack.enter_context(tc.psum_pool(name="psum", bufs=4))
        stack.enter_context(tc.manual_schedule())

        x_words = {}

        def load_x(c):
            n = LOAD_TILES[c]
            first = sum(LOAD_TILES[:c])
            x_rows = const.tile([P, n * K], BF16, name="x_rows%d" % c)
            halves = x_rows[:].rearrange("p (t s d) -> p t s d", t=n, s=2)
            for s in range(2):
                nc.sync.dma_start(out=halves[:, :, s, :], in_=x_views[s][:, first : first + n, :])
            for t in range(n):
                x_words[first + t] = (x_rows[:].bitcast(F32), t)

        load_x(0)
        w_words = []
        for j in range(F_TILES):
            w_rows = const.tile([P, K], BF16, name="w_rows%d" % j)
            nc.sync.dma_start(out=w_rows[:], in_=w_view[:, j, :])
            w_words.append(w_rows[:].bitcast(F32))
        for c in range(1, len(LOAD_TILES)):
            load_x(c)

        ones = const.tile([P, F], BF16)
        nc.vector.memset(ones[:], 1.0)
        bias_row = const.tile([P, F], BF16)
        nc.vector.memset(bias_row[:], 0.0)
        nc.scalar.dma_start(out=bias_row[0:1, :], in_=b1.rearrange("(o f) -> o f", o=1))
        unit = const.tile([P, 1], F32)
        nc.vector.memset(unit[:], 1.0)
        identity = const.tile([P, P], F32)
        make_identity(nc, identity[:])
        warm = const.tile([P, 1], F32)
        nc.scalar.activation(out=warm[:], in_=unit[:], func=ACT.Abs_reciprocal_sqrt)

        banks, grouped, codes, scales, product = {}, {}, {}, {}, {}
        hidden, row_sum, square_sum, rstd, shift, normed = {}, {}, {}, {}, {}, {}
        lift, finished = {}, {}

        def transpose(g):
            for b in range(SIZES[g] // 2):
                bank = psum.tile([P, 2, 2, P], F32, tag="words")
                for j in range(2):
                    words, t = x_words[FIRST[g] + 2 * b + j]
                    for u in range(2):
                        nc.tensor.transpose(
                            bank[:, j, u, :], words[:, t * HALF + u : (t + 1) * HALF : 2], identity[:]
                        )
                banks[(g, b)] = bank

        def regroup(g, b):
            if b == 0:
                grouped_new = work.tile([P, SIZES[g] * K], BF16, tag="grouped", align_bytes=64)
                grouped[g] = grouped_new
            words = grouped[g][:].bitcast(F32).rearrange("p (j r u) -> p j r u", j=SIZES[g], u=2)
            nc.scalar.copy(
                out=words[:, 2 * b : 2 * b + 2, :, :],
                in_=banks[(g, b)][:].rearrange("p j u r -> p j r u"),
            )

        def quantise(g):
            codes_new = work.tile([P, SIZES[g] * P], U32, tag="codes", align_bytes=64)
            scales_new = work.tile([P, SIZES[g] * P], U8, tag="scales", align_bytes=64)
            nc.vector.quantize_mx(
                out=codes_new[:].bitcast(FP8X4), scales=scales_new[:], in_=grouped[g][:]
            )
            codes[g] = codes_new
            scales[g] = scales_new

        def multiply(g, j):
            bank = psum.tile([P, F], F32, tag="product")
            nc.tensor.matmul_mx(
                out=bank[:],
                lhsT=codes[g][:, j * P : (j + 1) * P].bitcast(FP8X4),
                lhsT_scale=scales[g][:, j * P : (j + 1) * P],
                rhs=w_codes[:].bitcast(FP8X4),
                rhs_scale=w_scales[:],
                start=True,
                stop=True,
            )
            product[(g, j)] = bank

        def bias_add_order(g):
            tiles = list(range(SIZES[g]))
            return tiles if g < FILLING else tiles[-1:] + tiles[:-1]

        def add_bias(g, j):
            if g not in hidden:
                hidden_new = work.tile([P, SIZES[g], F], F32, tag="hidden", bufs=5)
                row_sum_new = stats.tile([P, SIZES[g]], F32, tag="row_sum")
                hidden[g] = hidden_new
                row_sum[g] = row_sum_new
            nc.vector.scalar_tensor_tensor(
                out=hidden[g][:, j, :],
                in0=product[(g, j)][:],
                scalar=1.0,
                in1=bias[:],
                op0=ALU.mult,
                op1=ALU.add,
                accum_out=row_sum[g][:, j : j + 1],
            )

        def sum_squares(g):
            square_sum_new = stats.tile([P, SIZES[g]], F32, tag="square_sum")
            square_sum[g] = square_sum_new
            order = bias_add_order(g)
            for j in order[-1:] + order[:-1]:
                squares = work.tile([P, F], BF16, tag="squares")
                nc.scalar.activation(
                    out=squares[:],
                    in_=hidden[g][:, j, :],
                    func=ACT.Square,
                    bias=row_sum[g][:, j : j + 1],
                    scale=-1.0 * F,
                    accum_out=square_sum[g][:, j : j + 1],
                )

        def reciprocal_std(g):
            rstd_new = stats.tile([P, SIZES[g]], F32, tag="rstd")
            nc.scalar.activation(
                out=rstd_new[:],
                in_=square_sum[g][:],
                func=ACT.Abs_reciprocal_sqrt,
                bias=EPS,
                scale=1.0 / (F * F * F),
            )
            rstd[g] = rstd_new

        def mean_shift(g):
            shift_new = stats.tile([P, SIZES[g]], F32, tag="shift")
            nc.vector.scalar_tensor_tensor(
                out=shift_new[:],
                in0=row_sum[g][:],
                scalar=-1.0 / F,
                in1=rstd[g][:],
                op0=ALU.mult,
                op1=ALU.mult,
            )
            shift[g] = shift_new

        def gpsimd_tiles(g):
            if SIZES[g] < 4 or g >= GROUPS - 4:
                return 0
            return 3 if g % 2 == 0 else 1

        def gpsimd_finishes(g):
            return gpsimd_tiles(g) == 3

        def normalise_gpsimd(g):
            normed_new = work.tile([P, SIZES[g], F], F32, tag="normed", bufs=4)
            normed[g] = normed_new
            for j in range(gpsimd_tiles(g)):
                nc.gpsimd.tensor_scalar(
                    out=normed[g][:, j, :],
                    in0=hidden[g][:, j, :],
                    scalar1=rstd[g][:, j : j + 1],
                    scalar2=shift[g][:, j : j + 1],
                    op0=ALU.mult,
                    op1=ALU.add,
                )

        def normalise_scalar(g):
            for j in range(gpsimd_tiles(g), SIZES[g]):
                nc.scalar.activation(
                    out=normed[g][:, j, :],
                    in_=hidden[g][:, j, :],
                    func=ACT.Identity,
                    bias=shift[g][:, j : j + 1],
                    scale=rstd[g][:, j : j + 1],
                )

        def lift_negatives(g):
            lift_new = work.tile([P, F], F32, tag="lift")
            lift[g] = lift_new
            nc.scalar.activation(
                out=lift[g][:], in_=normed[g][:, 0, :], func=ACT.Relu, scale=-(1.0 - SLOPE)
            )

        def finish_tile(g):
            finished_new = work.tile([P, F], F32, tag="finished")
            finished[g] = finished_new
            nc.gpsimd.tensor_tensor(
                out=finished[g][:], in0=normed[g][:, 0, :], in1=lift[g][:], op=ALU.add
            )

        def store(source, g, start, stop):
            nc.sync.dma_start(out=out_view[:, FIRST[g] * F + start : FIRST[g] * F + stop], in_=source)

        def leaky_and_store(g):
            result = work.tile([P, SIZES[g] * F], F32, tag="result", bufs=4)
            flat = normed[g][:].rearrange("p j f -> p (j f)")
            start = F if gpsimd_finishes(g) else 0
            width = SIZES[g] * F - start
            if g >= GROUPS - LAST_GROUPS:
                width = F
            if g == GROUPS - 1:
                width = F // 2
            for c in range(start, SIZES[g] * F, width):
                cols = slice(c, c + width)
                nc.vector.scalar_tensor_tensor(
                    out=result[:, cols],
                    in0=flat[:, cols],
                    scalar=SLOPE,
                    in1=flat[:, cols],
                    op0=ALU.mult,
                    op1=ALU.max,
                )
                store(result[:, cols], g, c, c + width)

        bias_bank = psum.tile([P, F], F32, tag="product")
        for n in range(WARM_UPS):
            nc.tensor.matmul(out=bias_bank[:], lhsT=ones[:, 0:P], rhs=ones[:], start=True, stop=True)
        transpose(0)
        regroup(0, 0)
        quantise(0)
        w_codes = const.tile([P, F], U32, align_bytes=64)
        w_scales = const.tile([P, F], U8, align_bytes=64)
        for j in range(F_TILES):
            w_bank = psum.tile([P, 2, P], F32, tag="words")
            for u in range(2):
                nc.tensor.transpose(w_bank[:, u, :], w_words[j][:, u::2], identity[:])
            w_grouped = work.tile([P, K], BF16, tag="w_grouped", align_bytes=64)
            nc.scalar.copy(
                out=w_grouped[:].bitcast(F32).rearrange("p (r u) -> p r u", u=2),
                in_=w_bank[:].rearrange("p u r -> p r u"),
            )
            cols = slice(j * P, (j + 1) * P)
            nc.vector.quantize_mx(
                out=w_codes[:, cols].bitcast(FP8X4), scales=w_scales[:, cols], in_=w_grouped[:]
            )
        nc.tensor.matmul(
            out=bias_bank[:], lhsT=ones[:, 0:P], rhs=bias_row[:], start=True, stop=True
        )
        bias = const.tile([P, F], F32)
        nc.vector.tensor_copy(out=bias[:], in_=bias_bank[:])
        transpose(1)
        transpose(2)

        def live(g):
            return 0 <= g < GROUPS

        transposed = 3
        for i in range(GROUPS + 8):
            if live(i) and i > 0:
                regroup(i, 0)
            if live(i - 4):
                reciprocal_std(i - 4)
            if live(i - 5):
                normalise_gpsimd(i - 5)
                if gpsimd_finishes(i - 5):
                    lift_negatives(i - 5)
            if live(i) and SIZES[i] > 2:
                regroup(i, 1)
            if live(i - 5):
                normalise_scalar(i - 5)
            if live(i - 6):
                leaky_and_store(i - 6)
                if gpsimd_finishes(i - 6):
                    finish_tile(i - 6)
            if live(i - 7) and gpsimd_finishes(i - 7):
                store(finished[i - 7][:], i - 7, 0, F)
            if live(i - 4):
                mean_shift(i - 4)
            if live(i - 1) and i > 1:
                quantise(i - 1)
            if live(i - 3):
                sum_squares(i - 3)
            order = bias_add_order(i - 2) if live(i - 2) else []
            if order and order[0] != 0:
                add_bias(i - 2, order[0])
            for j in range(4):
                if j in order and (j != order[0] or j == 0):
                    add_bias(i - 2, j)
                if live(i - 1) and j < SIZES[i - 1]:
                    multiply(i - 1, j)
            if i >= 1:
                while transposed < min(i + 3, GROUPS):
                    transpose(transposed)
                    transposed += 1
